import numpy as np
import ml_dtypes


def mxq(x, axis, fmt="e4m3"):
    dtype, down = {"e4m3": (ml_dtypes.float8_e4m3fn, 7), "e5m2": (ml_dtypes.float8_e5m2, 14)}[fmt]
    v = np.moveaxis(np.asarray(x, np.float32).astype(ml_dtypes.bfloat16).astype(np.float64), axis, -1)
    blocks = v.reshape(v.shape[:-1] + (-1, 32))
    amax = np.abs(blocks).max(-1, keepdims=True)
    byte = np.maximum(np.where(amax > 0, np.frexp(amax)[1] - 1 + 127, 0) - down, 1)
    scale = np.exp2(byte - 127.0)
    codes = (blocks / scale).astype(np.float32).astype(dtype).astype(np.float64)
    return np.moveaxis((codes * scale).reshape(v.shape), -1, axis)


WIDE = False


def mx_kscale(k):
    if not WIDE:
        return np.ones(k)
    levels = np.array([10, -10, 5, -5, 0])
    a = np.random.permutation(np.resize(levels, k // 512 * 4)).reshape(k // 512, 4)
    idx = np.arange(k)
    return np.exp2(a[idx // 512, idx % 128 // 32])


BF16 = ml_dtypes.bfloat16


def bf(x):
    return np.asarray(x, np.float32).astype(BF16)


def f64(x):
    return np.asarray(x).astype(np.float64)


E2M1 = np.array([0.0, 0.5, 1.0, 1.5, 2.0, 3.0, 4.0, 6.0, -0.0, -0.5, -1.0, -1.5, -2.0, -3.0, -4.0, -6.0])


def pack_weight(w, fmt):
    k, n = w.shape
    w = f64(bf(w)).reshape(k // 32, 32, n)
    amax = np.abs(w).max(1)
    if fmt == "e4m3":
        byte = np.frexp(amax)[1] - 1 + 127 - 7
    else:
        mant, ex = np.frexp(amax / 6.0)
        byte = np.where(mant > 0.5, ex, ex - 1) + 127
    byte = np.clip(np.where(amax > 0, byte, 1), 1, 254)
    scaled = (w * np.exp2(127.0 - byte)[:, None, :]).reshape(k, n).astype(np.float32)
    by_word = np.ascontiguousarray(scaled.reshape(k // 512, 128, 4, n).transpose(0, 1, 3, 2))
    if fmt == "e4m3":
        words = by_word.astype(ml_dtypes.float8_e4m3fn).view(np.uint8)
    else:
        c = by_word.astype(ml_dtypes.float4_e2m1fn).view(np.uint8) & 0xF
        words = c[..., 0::2] | (c[..., 1::2] << 4)
    return np.ascontiguousarray(words), np.ascontiguousarray(byte.astype(np.uint8).reshape(k // 512, 16, n))


def unpack_weight(words, scales, fmt):
    g, p, n, _ = words.shape
    if fmt == "e4m3":
        vals = np.ascontiguousarray(words).view(ml_dtypes.float8_e4m3fn).astype(np.float64)
    else:
        nib = np.empty((g, p, n, 4), np.uint8)
        nib[..., 0::2] = words & 0xF
        nib[..., 1::2] = words >> 4
        vals = E2M1[nib]
    vals = vals * np.repeat(np.exp2(scales.astype(np.float64) - 127.0), 8, axis=1)[..., None]
    return vals.transpose(0, 1, 3, 2).reshape(g * 512, n)


B, S, H, R = 16, 384, 512, 3
N = S // R
FMT = "e4m3"


def setup_inputs():
    t = mx_kscale(H)
    h = bf(np.random.standard_normal((B, N, R, H)))
    w1 = np.random.standard_normal((H, H)) / np.sqrt(H) * t[:, None]
    b1 = bf(np.random.standard_normal(H) * 0.3 * t)
    w2 = np.random.standard_normal((H, H)) * 2.0 / np.sqrt(H) / t[None, :]
    w1_words, w1_scales = pack_weight(np.ascontiguousarray(w1.T), FMT)
    w2_words, w2_scales = pack_weight(np.ascontiguousarray(w2.T), FMT)
    return {"h": h,
            "s2t_W1_w_words": w1_words,
            "s2t_W1_w_scales": w1_scales,
            "s2t_W1_b": b1,
            "s2t_W_w_words": w2_words,
            "s2t_W_w_scales": w2_scales}


def reference(h, s2t_W1_w_words, s2t_W1_w_scales, s2t_W1_b, s2t_W_w_words, s2t_W_w_scales):
    hf = f64(h)
    rows = hf.reshape(B * N * R, H)
    f = np.maximum((mxq(rows, 1, "e4m3") @ unpack_weight(s2t_W1_w_words, s2t_W1_w_scales, FMT)) + f64(s2t_W1_b), 0.0)
    z = (mxq(f, 1, "e4m3") @ unpack_weight(s2t_W_w_words, s2t_W_w_scales, FMT)).reshape(B, N, R, H)
    e = np.exp(z - z.max(-2, keepdims=True))
    p = e / e.sum(-2, keepdims=True)
    return (p * hf).sum(-2)

@@ -1,0 +1,252 @@
+import concourse.mybir as mybir
+from concourse.masks import make_identity
+
+F32 = mybir.dt.float32
+BF16 = mybir.dt.bfloat16
+I32 = mybir.dt.int32
+U32 = mybir.dt.uint32
+U8 = mybir.dt.uint8
+FP8X4 = mybir.dt.float8_e4m3fn_x4
+AF = mybir.ActivationFunctionType
+ALU = mybir.AluOpType
+
+P = 128
+H = 512
+R = 3
+N_BLOCKS = 16 * 128
+N_GROUPS = N_BLOCKS // P
+WORDS = H // 2
+
+FLOPS = 2 * 2 * N_BLOCKS * R * H * H
+
+
+def by_word_half(ap):
+    return ap.rearrange("b (p u e) -> b u p e", u=2, e=2)
+
+
+def sorted_halves(ap):
+    return ap.rearrange("b (u p e) -> b u p e", u=2, e=2)
+
+
+def load_weight(nc, pool, words, scales, name):
+    codes = pool.tile([P, H], U32, name=name + "_codes", align_bytes=64)
+    plane = pool.tile([P, H], U8, name=name + "_plane", align_bytes=64)
+    nc.vector.memset(plane[:].bitcast(I32), 0)
+    nc.sync.dma_start(
+        out=codes[:].bitcast(I32), in_=words[0].rearrange("p n t -> p (n t)").bitcast(I32)
+    )
+    for quadrant in range(4):
+        nc.sync.dma_start(
+            out=plane[32 * quadrant : 32 * quadrant + 4, :].bitcast(I32),
+            in_=scales[0, 4 * quadrant : 4 * quadrant + 4, :].bitcast(I32),
+        )
+    return codes, plane
+
+
+def tile_blocksa_pa_t_kernel(
+    tc, h, s2t_W1_w_words, s2t_W1_w_scales, s2t_W1_b, s2t_W_w_words, s2t_W_w_scales, out
+):
+    nc = tc.nc
+    h_groups = h.rearrange("b n r c -> (b n) r c").rearrange("(p g) r c -> p g r c", g=N_GROUPS)
+    out_groups = out.rearrange("b n c -> (b n) c").rearrange("(p g) c -> p g c", g=N_GROUPS)
+
+    with (
+        tc.tile_pool(name="keep", bufs=1) as keep,
+        tc.tile_pool(name="work", bufs=2) as work,
+        tc.tile_pool(name="single", bufs=1) as single,
+        tc.psum_pool(name="psum_x", bufs=3) as psum_x,
+        tc.psum_pool(name="psum_z", bufs=2) as psum_z,
+        tc.psum_pool(name="psum_turn", bufs=3) as psum_turn,
+        tc.manual_schedule(),
+    ):
+        ident = keep.tile([P, P], F32, name="ident")
+        make_identity(nc, ident[:])
+        half = keep.tile([P, 1], F32, name="half")
+        nc.vector.memset(half[:], 0.5)
+
+        h_sb = [keep.tile([P, R, H], BF16, name="h%d" % g) for g in range(N_GROUPS)]
+        nc.sync.dma_start(out=h_sb[0][:], in_=h_groups[:, 0])
+        w1_codes, w1_plane = load_weight(nc, keep, s2t_W1_w_words, s2t_W1_w_scales, "w1")
+        bias_rows = keep.tile([P, H], BF16, name="bias_rows")
+        nc.sync.dma_start(out=bias_rows[:], in_=s2t_W1_b.partition_broadcast(P))
+        nc.sync.dma_start(out=h_sb[1][:], in_=h_groups[:, 1])
+        w2_codes, w2_plane = load_weight(nc, keep, s2t_W_w_words, s2t_W_w_scales, "w2")
+        for g in range(2, N_GROUPS):
+            nc.sync.dma_start(out=h_sb[g][:], in_=h_groups[:, g])
+        bias_sorted = keep.tile([P, H], F32, name="bias_sorted")
+        nc.gpsimd.tensor_copy(out=sorted_halves(bias_sorted[:]), in_=by_word_half(bias_rows[:]))
+
+        abs_tanh = [keep.tile([P, H], F32, name="abs_tanh%d" % g) for g in range(N_GROUPS)]
+        logit2 = [keep.tile([P, H], F32, name="logit2_%d" % g) for g in range(N_GROUPS)]
+        rest = [keep.tile([P, H], F32, name="rest%d" % g) for g in range(N_GROUPS)]
+
+        h_grouped, h_codes, h_scales, x_psum = {}, {}, {}, {}
+        f_grouped, f_codes, f_scales, z_psum = {}, {}, {}, {}
+        z1_sbuf, diff01, tanh1, h0_minus_h1, h2_minus_h1, mix = {}, {}, {}, {}, {}, {}
+
+        def transpose_words(words, r):
+            turned = psum_turn.tile([P, 2, P], F32, name="turned", tag="turn")
+            for u in range(2):
+                nc.tensor.transpose(out=turned[:, u, :], in_=words(r, u), identity=ident[:])
+            return turned
+
+        def turn_h(g):
+            h_words = h_sb[g][:].bitcast(F32)
+            h_grouped[g] = work.tile([P, R, 4 * P], BF16, name="h_grouped", align_bytes=64)
+            for r in range(R):
+                turned = transpose_words(lambda r, u: h_words[:, r, u:WORDS:2], r)
+                nc.scalar.copy(
+                    out=h_grouped[g][:, r, :].bitcast(F32).rearrange("p (b u) -> p b u", u=2),
+                    in_=turned[:].rearrange("p u b -> p b u"),
+                )
+
+        def quantise(grouped, name):
+            codes = work.tile([P, R, P], U32, name=name + "_codes", align_bytes=64)
+            scales = work.tile([P, R, P], U8, name=name + "_scales", align_bytes=64)
+            for r in range(R):
+                nc.vector.quantize_mx(
+                    out=codes[:, r, :].bitcast(FP8X4), scales=scales[:, r, :], in_=grouped[:, r, :]
+                )
+            return codes, scales
+
+        def product(acc, codes, scales, r, w_codes, w_plane):
+            nc.tensor.matmul_mx(
+                out=acc[:],
+                lhsT=codes[:, r, :].bitcast(FP8X4),
+                lhsT_scale=scales[:, r, :],
+                rhs=w_codes[:].bitcast(FP8X4),
+                rhs_scale=w_plane[:],
+                start=True,
+                stop=True,
+            )
+
+        def first_matmul(g):
+            h_codes[g], h_scales[g] = quantise(h_grouped[g], "h")
+            x_psum[g] = []
+            for r in range(R):
+                x_psum[g].append(psum_x.tile([P, H], F32, name="x", tag="x"))
+                product(x_psum[g][r], h_codes[g], h_scales[g], r, w1_codes, w1_plane)
+
+        def hidden_layer(g):
+            pre_relu = work.tile([P, R, H], BF16, name="pre_relu")
+            f_grouped[g] = work.tile([P, R, 4 * P], BF16, name="f_grouped", align_bytes=64)
+            pre_words = pre_relu[:].bitcast(F32)
+            for r in range(R):
+                nc.vector.tensor_tensor(
+                    out=sorted_halves(pre_relu[:, r, :]),
+                    in0=by_word_half(x_psum[g][r][:]),
+                    in1=sorted_halves(bias_sorted[:]),
+                    op=ALU.add,
+                )
+                turned = transpose_words(lambda r, u: pre_words[:, r, u * P : (u + 1) * P], r)
+                nc.scalar.activation(
+                    out=f_grouped[g][:, r, :].rearrange("p (b u e) -> p b u e", u=2, e=2),
+                    in_=turned[:]
+                    .rearrange("p u b -> p (u b)")
+                    .bitcast(BF16)
+                    .rearrange("p (u b e) -> p b u e", u=2, e=2),
+                    func=AF.Relu,
+                )
+
+        def second_matmul(g):
+            f_codes[g], f_scales[g] = quantise(f_grouped[g], "f")
+            z1 = psum_turn.tile([P, H], F32, name="z1", tag="turn")
+            z0 = psum_z.tile([P, H], F32, name="z0", tag="z")
+            z2 = psum_z.tile([P, H], F32, name="z2", tag="z")
+            z_psum[g] = [z0, z1, z2]
+            for r in (1, 0, 2):
+                product(z_psum[g][r], f_codes[g], f_scales[g], r, w2_codes, w2_plane)
+
+        def copy_z1(g):
+            z1_sbuf[g] = work.tile([P, H], F32, name="z1_sbuf")
+            nc.scalar.copy(out=z1_sbuf[g][:], in_=z_psum[g][1][:])
+
+        def compare_logits(g):
+            z0, z2 = z_psum[g][0], z_psum[g][2]
+            larger = work.tile([P, H], F32, name="larger")
+            diff01[g] = work.tile([P, H], F32, name="diff01")
+            nc.vector.tensor_tensor(out=larger[:], in0=z0[:], in1=z1_sbuf[g][:], op=ALU.max)
+            nc.vector.tensor_tensor(out=diff01[g][:], in0=z0[:], in1=z1_sbuf[g][:], op=ALU.subtract)
+            nc.vector.tensor_tensor(out=logit2[g][:], in0=z2[:], in1=larger[:], op=ALU.subtract)
+
+        def first_tanh(g):
+            tanh1[g] = work.tile([P, H], F32, name="tanh1")
+            nc.scalar.activation(out=tanh1[g][:], in_=diff01[g][:], func=AF.Tanh, scale=0.5)
+            nc.scalar.activation(out=abs_tanh[g][:], in_=tanh1[g][:], func=AF.Abs)
+
+        def differences_of_h(g):
+            h2_minus_h1[g] = single.tile([P, H], F32, name="h2_minus_h1")
+            nc.gpsimd.tensor_tensor(
+                out=h2_minus_h1[g][:], in0=h_sb[g][:, 2, :], in1=h_sb[g][:, 1, :], op=ALU.subtract
+            )
+            h0_minus_h1[g] = single.tile([P, H], F32, name="h0_minus_h1")
+            nc.gpsimd.tensor_tensor(
+                out=h0_minus_h1[g][:], in0=h_sb[g][:, 0, :], in1=h_sb[g][:, 1, :], op=ALU.subtract
+            )
+
+        def mix_tokens_0_and_1(g):
+            mix[g] = work.tile([P, H], F32, name="mix")
+            nc.vector.scalar_tensor_tensor(
+                out=mix[g][:],
+                in0=tanh1[g][:],
+                scalar=1.0,
+                in1=h0_minus_h1[g][:],
+                op0=ALU.add,
+                op1=ALU.mult,
+            )
+
+        def distance_to_token_2(g):
+            nc.vector.scalar_tensor_tensor(
+                out=rest[g][:],
+                in0=mix[g][:],
+                scalar=-0.5,
+                in1=h2_minus_h1[g][:],
+                op0=ALU.mult,
+                op1=ALU.add,
+            )
+
+        def run(stage, g):
+            if 0 <= g < N_GROUPS:
+                stage(g)
+
+        for t in range(-1, N_GROUPS + 3):
+            run(turn_h, t + 1)
+            run(first_matmul, t)
+            run(mix_tokens_0_and_1, t - 3)
+            run(second_matmul, t - 1)
+            run(distance_to_token_2, t - 3)
+            run(first_tanh, t - 2)
+            run(copy_z1, t - 1)
+            run(hidden_layer, t)
+            run(compare_logits, t - 1)
+            run(differences_of_h, t - 2)
+
+        for g in range(N_GROUPS):
+            nc.scalar.activation(
+                out=abs_tanh[g][:], in_=abs_tanh[g][:], func=AF.Ln, scale=0.5, bias=half[:]
+            )
+        for g in range(N_GROUPS):
+            nc.vector.tensor_tensor(
+                out=logit2[g][:], in0=logit2[g][:], in1=abs_tanh[g][:], op=ALU.add
+            )
+            nc.scalar.activation(out=logit2[g][:], in_=logit2[g][:], func=AF.Tanh, scale=0.5)
+        for g in range(N_GROUPS + 1):
+            if g < N_GROUPS:
+                nc.vector.scalar_tensor_tensor(
+                    out=rest[g][:],
+                    in0=logit2[g][:],
+                    scalar=-1.0,
+                    in1=rest[g][:],
+                    op0=ALU.add,
+                    op1=ALU.mult,
+                )
+            if g >= 1:
+                nc.vector.scalar_tensor_tensor(
+                    out=rest[g - 1][:],
+                    in0=rest[g - 1][:],
+                    scalar=0.5,
+                    in1=h_sb[g - 1][:, 2, :],
+                    op0=ALU.mult,
+                    op1=ALU.add,
+                )
+                nc.sync.dma_start(out=out_groups[:, g - 1, :], in_=rest[g - 1][:])

@@ -63,6 +63,10 @@ def tile_blocksa_pa_t_kernel(
         make_identity(nc, ident[:])
         half = keep.tile([P, 1], F32, name="half")
         nc.vector.memset(half[:], 0.5)
+        plus_half = keep.tile([P, P], BF16, name="plus_half")
+        minus_half = keep.tile([P, P], BF16, name="minus_half")
+        nc.vector.tensor_scalar_mul(out=plus_half[:], in0=ident[:], scalar1=0.5)
+        nc.vector.tensor_scalar_mul(out=minus_half[:], in0=ident[:], scalar1=-0.5)
 
         h_sb = [keep.tile([P, R, H], BF16, name="h%d" % g) for g in range(N_GROUPS)]
         nc.sync.dma_start(out=h_sb[0][:], in_=h_groups[:, 0])
@@ -82,7 +86,7 @@ def tile_blocksa_pa_t_kernel(
 
         h_grouped, h_codes, h_scales, x_psum = {}, {}, {}, {}
         f_grouped, f_codes, f_scales, z_psum = {}, {}, {}, {}
-        z1_sbuf, diff01, tanh1, h0_minus_h1, h2_minus_h1, mix = {}, {}, {}, {}, {}, {}
+        z1_sbuf, diff01, tanh1, half_h0_minus_h1, h2_minus_h1, mix = {}, {}, {}, {}, {}, {}
 
         def transpose_words(words, r):
             turned = psum_turn.tile([P, 2, P], F32, name="turned", tag="turn")
@@ -148,8 +152,10 @@ def tile_blocksa_pa_t_kernel(
                     func=AF.Relu,
                 )
 
-        def second_matmul(g):
+        def quantise_f(g):
             f_codes[g], f_scales[g] = quantise(f_grouped[g], "f")
+
+        def second_matmul(g):
             z1 = psum_turn.tile([P, H], F32, name="z1", tag="turn")
             z0 = psum_z.tile([P, H], F32, name="z0", tag="z")
             z2 = psum_z.tile([P, H], F32, name="z2", tag="z")
@@ -174,14 +180,13 @@ def tile_blocksa_pa_t_kernel(
             nc.scalar.activation(out=tanh1[g][:], in_=diff01[g][:], func=AF.Tanh, scale=0.5)
             nc.scalar.activation(out=abs_tanh[g][:], in_=tanh1[g][:], func=AF.Abs)
 
-        def differences_of_h(g):
-            h2_minus_h1[g] = single.tile([P, H], F32, name="h2_minus_h1")
-            nc.gpsimd.tensor_tensor(
-                out=h2_minus_h1[g][:], in0=h_sb[g][:, 2, :], in1=h_sb[g][:, 1, :], op=ALU.subtract
+        def half_difference_0_1(g):
+            half_h0_minus_h1[g] = psum_z.tile([P, H], F32, name="half_h0_minus_h1", tag="z")
+            nc.tensor.matmul(
+                out=half_h0_minus_h1[g][:], lhsT=plus_half[:], rhs=h_sb[g][:, 0, :], start=True, stop=False
             )
-            h0_minus_h1[g] = single.tile([P, H], F32, name="h0_minus_h1")
-            nc.gpsimd.tensor_tensor(
-                out=h0_minus_h1[g][:], in0=h_sb[g][:, 0, :], in1=h_sb[g][:, 1, :], op=ALU.subtract
+            nc.tensor.matmul(
+                out=half_h0_minus_h1[g][:], lhsT=minus_half[:], rhs=h_sb[g][:, 1, :], start=False, stop=True
             )
 
         def mix_tokens_0_and_1(g):
@@ -190,19 +195,20 @@ def tile_blocksa_pa_t_kernel(
                 out=mix[g][:],
                 in0=tanh1[g][:],
                 scalar=1.0,
-                in1=h0_minus_h1[g][:],
+                in1=half_h0_minus_h1[g][:],
                 op0=ALU.add,
                 op1=ALU.mult,
             )
 
         def distance_to_token_2(g):
-            nc.vector.scalar_tensor_tensor(
-                out=rest[g][:],
-                in0=mix[g][:],
-                scalar=-0.5,
-                in1=h2_minus_h1[g][:],
-                op0=ALU.mult,
-                op1=ALU.add,
+            nc.gpsimd.tensor_tensor(
+                out=rest[g][:], in0=h2_minus_h1[g][:], in1=mix[g][:], op=ALU.subtract
+            )
+
+        def difference_2_1(g):
+            h2_minus_h1[g] = single.tile([P, H], F32, name="h2_minus_h1")
+            nc.gpsimd.tensor_tensor(
+                out=h2_minus_h1[g][:], in0=h_sb[g][:, 2, :], in1=h_sb[g][:, 1, :], op=ALU.subtract
             )
 
         def run(stage, g):
@@ -210,16 +216,18 @@ def tile_blocksa_pa_t_kernel(
                 stage(g)
 
         for t in range(-1, N_GROUPS + 3):
-            run(turn_h, t + 1)
+            run(first_tanh, t - 2)
             run(first_matmul, t)
+            run(quantise_f, t - 1)
             run(mix_tokens_0_and_1, t - 3)
             run(second_matmul, t - 1)
-            run(distance_to_token_2, t - 3)
-            run(first_tanh, t - 2)
             run(copy_z1, t - 1)
+            run(distance_to_token_2, t - 3)
+            run(difference_2_1, t - 2)
+            run(turn_h, t + 1)
             run(hidden_layer, t)
             run(compare_logits, t - 1)
-            run(differences_of_h, t - 2)
+            run(half_difference_0_1, t - 2)
 
         for g in range(N_GROUPS):
             nc.scalar.activation(

@@ -155,12 +155,14 @@ def tile_blocksa_pa_t_kernel(
         def quantise_f(g):
             f_codes[g], f_scales[g] = quantise(f_grouped[g], "f")
 
-        def second_matmul(g):
+        def second_matmul_token_1(g):
             z1 = psum_turn.tile([P, H], F32, name="z1", tag="turn")
-            z0 = psum_z.tile([P, H], F32, name="z0", tag="z")
-            z2 = psum_z.tile([P, H], F32, name="z2", tag="z")
-            z_psum[g] = [z0, z1, z2]
-            for r in (1, 0, 2):
+            z_psum[g] = {1: z1}
+            product(z1, f_codes[g], f_scales[g], 1, w2_codes, w2_plane)
+
+        def second_matmul_tokens_0_and_2(g):
+            for r in (0, 2):
+                z_psum[g][r] = psum_z.tile([P, H], F32, name="z%d" % r, tag="z")
                 product(z_psum[g][r], f_codes[g], f_scales[g], r, w2_codes, w2_plane)
 
         def copy_z1(g):
@@ -220,11 +222,12 @@ def tile_blocksa_pa_t_kernel(
             run(first_matmul, t)
             run(quantise_f, t - 1)
             run(mix_tokens_0_and_1, t - 3)
-            run(second_matmul, t - 1)
+            run(second_matmul_token_1, t - 1)
             run(copy_z1, t - 1)
             run(distance_to_token_2, t - 3)
             run(difference_2_1, t - 2)
             run(turn_h, t + 1)
+            run(second_matmul_tokens_0_and_2, t - 1)
             run(hidden_layer, t)
             run(compare_logits, t - 1)
             run(half_difference_0_1, t - 2)

@@ -59,26 +59,32 @@ def tile_blocksa_pa_t_kernel(
         tc.psum_pool(name="psum_turn", bufs=3) as psum_turn,
         tc.manual_schedule(),
     ):
-        ident = keep.tile([P, P], F32, name="ident")
-        make_identity(nc, ident[:])
-        half = keep.tile([P, 1], F32, name="half")
-        nc.vector.memset(half[:], 0.5)
-        plus_half = keep.tile([P, P], BF16, name="plus_half")
-        minus_half = keep.tile([P, P], BF16, name="minus_half")
-        nc.vector.tensor_scalar_mul(out=plus_half[:], in0=ident[:], scalar1=0.5)
-        nc.vector.tensor_scalar_mul(out=minus_half[:], in0=ident[:], scalar1=-0.5)
-
         h_sb = [keep.tile([P, R, H], BF16, name="h%d" % g) for g in range(N_GROUPS)]
         nc.sync.dma_start(out=h_sb[0][:], in_=h_groups[:, 0])
         w1_codes, w1_plane = load_weight(nc, keep, s2t_W1_w_words, s2t_W1_w_scales, "w1")
-        bias_rows = keep.tile([P, H], BF16, name="bias_rows")
-        nc.sync.dma_start(out=bias_rows[:], in_=s2t_W1_b.partition_broadcast(P))
         nc.sync.dma_start(out=h_sb[1][:], in_=h_groups[:, 1])
         w2_codes, w2_plane = load_weight(nc, keep, s2t_W_w_words, s2t_W_w_scales, "w2")
         for g in range(2, N_GROUPS):
             nc.sync.dma_start(out=h_sb[g][:], in_=h_groups[:, g])
+
+        bias_row = keep.tile([P, H], BF16, name="bias_row")
+        nc.vector.memset(bias_row[:], 0.0)
+        nc.scalar.dma_start(out=bias_row[0:1, :], in_=s2t_W1_b.unsqueeze(0))
+        ones = keep.tile([P, P], BF16, name="ones")
+        nc.vector.memset(ones[:], 1.0)
+        bias_psum = psum_x.tile([P, H], F32, name="bias_psum", tag="x")
+        nc.tensor.matmul(out=bias_psum[:], lhsT=ones[:], rhs=bias_row[:], start=True, stop=True)
         bias_sorted = keep.tile([P, H], F32, name="bias_sorted")
-        nc.gpsimd.tensor_copy(out=sorted_halves(bias_sorted[:]), in_=by_word_half(bias_rows[:]))
+        nc.vector.tensor_copy(out=sorted_halves(bias_sorted[:]), in_=by_word_half(bias_psum[:]))
+
+        half = keep.tile([P, 1], F32, name="half")
+        nc.vector.memset(half[:], 0.5)
+        ident = keep.tile([P, P], F32, name="ident")
+        make_identity(nc, ident[:])
+        plus_half = keep.tile([P, P], BF16, name="plus_half")
+        minus_half = keep.tile([P, P], BF16, name="minus_half")
+        nc.vector.tensor_scalar_mul(out=plus_half[:], in0=ident[:], scalar1=0.5)
+        nc.vector.tensor_scalar_mul(out=minus_half[:], in0=ident[:], scalar1=-0.5)
 
         abs_tanh = [keep.tile([P, H], F32, name="abs_tanh%d" % g) for g in range(N_GROUPS)]
         logit2 = [keep.tile([P, H], F32, name="logit2_%d" % g) for g in range(N_GROUPS)]
@@ -155,14 +161,12 @@ def tile_blocksa_pa_t_kernel(
         def quantise_f(g):
             f_codes[g], f_scales[g] = quantise(f_grouped[g], "f")
 
-        def second_matmul_token_1(g):
+        def second_matmul(g):
             z1 = psum_turn.tile([P, H], F32, name="z1", tag="turn")
-            z_psum[g] = {1: z1}
-            product(z1, f_codes[g], f_scales[g], 1, w2_codes, w2_plane)
-
-        def second_matmul_tokens_0_and_2(g):
-            for r in (0, 2):
-                z_psum[g][r] = psum_z.tile([P, H], F32, name="z%d" % r, tag="z")
+            z0 = psum_z.tile([P, H], F32, name="z0", tag="z")
+            z2 = psum_z.tile([P, H], F32, name="z2", tag="z")
+            z_psum[g] = [z0, z1, z2]
+            for r in (1, 0, 2):
                 product(z_psum[g][r], f_codes[g], f_scales[g], r, w2_codes, w2_plane)
 
         def copy_z1(g):
@@ -222,12 +226,11 @@ def tile_blocksa_pa_t_kernel(
             run(first_matmul, t)
             run(quantise_f, t - 1)
             run(mix_tokens_0_and_1, t - 3)
-            run(second_matmul_token_1, t - 1)
+            run(second_matmul, t - 1)
             run(copy_z1, t - 1)
             run(distance_to_token_2, t - 3)
             run(difference_2_1, t - 2)
             run(turn_h, t + 1)
-            run(second_matmul_tokens_0_and_2, t - 1)
             run(hidden_layer, t)
             run(compare_logits, t - 1)
             run(half_difference_0_1, t - 2)

@@ -20,14 +20,6 @@ WORDS = H // 2
 FLOPS = 2 * 2 * N_BLOCKS * R * H * H
 
 
-def by_word_half(ap):
-    return ap.rearrange("b (p u e) -> b u p e", u=2, e=2)
-
-
-def sorted_halves(ap):
-    return ap.rearrange("b (u p e) -> b u p e", u=2, e=2)
-
-
 def load_weight(nc, pool, words, scales, name):
     codes = pool.tile([P, H], U32, name=name + "_codes", align_bytes=64)
     plane = pool.tile([P, H], U8, name=name + "_plane", align_bytes=64)
@@ -55,8 +47,8 @@ def tile_blocksa_pa_t_kernel(
         tc.tile_pool(name="work", bufs=2) as work,
         tc.tile_pool(name="single", bufs=1) as single,
         tc.psum_pool(name="psum_x", bufs=3) as psum_x,
-        tc.psum_pool(name="psum_z", bufs=2) as psum_z,
-        tc.psum_pool(name="psum_turn", bufs=3) as psum_turn,
+        tc.psum_pool(name="psum_z", bufs=1) as psum_z,
+        tc.psum_pool(name="psum_turn", bufs=1) as psum_turn,
         tc.manual_schedule(),
     ):
         h_sb = [keep.tile([P, R, H], BF16, name="h%d" % g) for g in range(N_GROUPS)]
@@ -67,15 +59,12 @@ def tile_blocksa_pa_t_kernel(
         for g in range(2, N_GROUPS):
             nc.sync.dma_start(out=h_sb[g][:], in_=h_groups[:, g])
 
-        bias_row = keep.tile([P, H], BF16, name="bias_row")
-        nc.vector.memset(bias_row[:], 0.0)
-        nc.scalar.dma_start(out=bias_row[0:1, :], in_=s2t_W1_b.unsqueeze(0))
-        ones = keep.tile([P, P], BF16, name="ones")
-        nc.vector.memset(ones[:], 1.0)
-        bias_psum = psum_x.tile([P, H], F32, name="bias_psum", tag="x")
-        nc.tensor.matmul(out=bias_psum[:], lhsT=ones[:], rhs=bias_row[:], start=True, stop=True)
-        bias_sorted = keep.tile([P, H], F32, name="bias_sorted")
-        nc.vector.tensor_copy(out=sorted_halves(bias_sorted[:]), in_=by_word_half(bias_psum[:]))
+        bias_bf16 = keep.tile([P, 4], BF16, name="bias_bf16")
+        nc.scalar.dma_start(out=bias_bf16[:], in_=s2t_W1_b.rearrange("(p t) -> p t", t=4))
+        bias = keep.tile([P, 4], F32, name="bias")
+        nc.vector.tensor_copy(out=bias[:], in_=bias_bf16[:])
+        bias_grouped = keep.tile([P, P, 4], F32, name="bias_grouped")
+        nc.vector.tensor_copy(out=bias_grouped[:], in_=bias[:].unsqueeze(1).to_broadcast([P, P, 4]))
 
         half = keep.tile([P, 1], F32, name="half")
         nc.vector.memset(half[:], 0.5)
@@ -86,29 +75,48 @@ def tile_blocksa_pa_t_kernel(
         nc.vector.tensor_scalar_mul(out=plus_half[:], in0=ident[:], scalar1=0.5)
         nc.vector.tensor_scalar_mul(out=minus_half[:], in0=ident[:], scalar1=-0.5)
 
+        w1_turned = keep.tile([P, H], U32, name="w1_turned", align_bytes=64)
+        w1_turned_plane = keep.tile([P, H], U8, name="w1_turned_plane", align_bytes=64)
+        nc.vector.tensor_copy(
+            out=w1_turned[:].bitcast(I32).rearrange("p (t m) -> p t m", t=4),
+            in_=w1_codes[:].bitcast(I32).rearrange("p (m t) -> p t m", t=4),
+        )
+        nc.vector.tensor_copy(
+            out=w1_turned_plane[:].rearrange("p (t m) -> p m t", t=4),
+            in_=w1_plane[:].rearrange("p (m t) -> p m t", t=4),
+        )
+
         abs_tanh = [keep.tile([P, H], F32, name="abs_tanh%d" % g) for g in range(N_GROUPS)]
         logit2 = [keep.tile([P, H], F32, name="logit2_%d" % g) for g in range(N_GROUPS)]
         rest = [keep.tile([P, H], F32, name="rest%d" % g) for g in range(N_GROUPS)]
 
         h_grouped, h_codes, h_scales, x_psum = {}, {}, {}, {}
-        f_grouped, f_codes, f_scales, z_psum = {}, {}, {}, {}
-        z1_sbuf, diff01, tanh1, half_h0_minus_h1, h2_minus_h1, mix = {}, {}, {}, {}, {}, {}
+        turned_01, turned_2 = {}, {}
+        f_pre, f_planes, f_grouped, f_codes, f_scales = {}, {}, {}, {}, {}
+        z0_minus_z1, z2_minus_z1 = {}, {}
+        relu01, tanh1, half_h0_minus_h1, h2_minus_h1, mix = {}, {}, {}, {}, {}
 
-        def transpose_words(words, r):
-            turned = psum_turn.tile([P, 2, P], F32, name="turned", tag="turn")
-            for u in range(2):
-                nc.tensor.transpose(out=turned[:, u, :], in_=words(r, u), identity=ident[:])
-            return turned
-
-        def turn_h(g):
+        def transpose_h(g):
             h_words = h_sb[g][:].bitcast(F32)
-            h_grouped[g] = work.tile([P, R, 4 * P], BF16, name="h_grouped", align_bytes=64)
+            turned_01[g] = psum_turn.tile([P, 2, 2, P], F32, name="turned_01")
+            turned_2[g] = psum_turn.tile([P, 2, P], F32, name="turned_2")
             for r in range(R):
-                turned = transpose_words(lambda r, u: h_words[:, r, u:WORDS:2], r)
-                nc.scalar.copy(
-                    out=h_grouped[g][:, r, :].bitcast(F32).rearrange("p (b u) -> p b u", u=2),
-                    in_=turned[:].rearrange("p u b -> p b u"),
-                )
+                turned = turned_01[g][:, r] if r < 2 else turned_2[g][:]
+                for u in range(2):
+                    nc.tensor.transpose(
+                        out=turned[:, u, :], in_=h_words[:, r, u:WORDS:2], identity=ident[:]
+                    )
+
+        def group_h(g):
+            h_grouped[g] = work.tile([P, R, 4 * P], BF16, name="h_grouped", align_bytes=64)
+            nc.scalar.copy(
+                out=h_grouped[g][:, 0:2, :].bitcast(F32).rearrange("p r (b u) -> p r b u", u=2),
+                in_=turned_01[g][:].rearrange("p r u b -> p r b u"),
+            )
+            nc.scalar.copy(
+                out=h_grouped[g][:, 2, :].bitcast(F32).rearrange("p (b u) -> p b u", u=2),
+                in_=turned_2[g][:].rearrange("p u b -> p b u"),
+            )
 
         def quantise(grouped, name):
             codes = work.tile([P, R, P], U32, name=name + "_codes", align_bytes=64)
@@ -119,75 +127,107 @@ def tile_blocksa_pa_t_kernel(
                 )
             return codes, scales
 
-        def product(acc, codes, scales, r, w_codes, w_plane):
+        def add_product(acc, g, r, start):
+            codes, scales = f_codes[g], f_scales[g]
             nc.tensor.matmul_mx(
                 out=acc[:],
                 lhsT=codes[:, r, :].bitcast(FP8X4),
                 lhsT_scale=scales[:, r, :],
-                rhs=w_codes[:].bitcast(FP8X4),
-                rhs_scale=w_plane[:],
-                start=True,
-                stop=True,
+                rhs=w2_codes[:].bitcast(FP8X4),
+                rhs_scale=w2_plane[:],
+                start=start,
+                stop=not start,
             )
 
-        def first_matmul(g):
+        def quantise_h(g):
             h_codes[g], h_scales[g] = quantise(h_grouped[g], "h")
+
+        def first_matmul(g):
             x_psum[g] = []
             for r in range(R):
-                x_psum[g].append(psum_x.tile([P, H], F32, name="x", tag="x"))
-                product(x_psum[g][r], h_codes[g], h_scales[g], r, w1_codes, w1_plane)
+                x_psum[g].append(psum_x.tile([P, 4, P], F32, name="x", tag="x"))
+                for t in range(4):
+                    nc.tensor.matmul_mx(
+                        out=x_psum[g][r][:, t, :],
+                        lhsT=w1_turned[:, t * P : (t + 1) * P].bitcast(FP8X4),
+                        lhsT_scale=w1_turned_plane[:, t * P : (t + 1) * P],
+                        rhs=h_codes[g][:, r, :].bitcast(FP8X4),
+                        rhs_scale=h_scales[g][:, r, :],
+                        start=True,
+                        stop=True,
+                    )
 
-        def hidden_layer(g):
-            pre_relu = work.tile([P, R, H], BF16, name="pre_relu")
-            f_grouped[g] = work.tile([P, R, 4 * P], BF16, name="f_grouped", align_bytes=64)
-            pre_words = pre_relu[:].bitcast(F32)
-            for r in range(R):
-                nc.vector.tensor_tensor(
-                    out=sorted_halves(pre_relu[:, r, :]),
-                    in0=by_word_half(x_psum[g][r][:]),
-                    in1=sorted_halves(bias_sorted[:]),
-                    op=ALU.add,
-                )
-                turned = transpose_words(lambda r, u: pre_words[:, r, u * P : (u + 1) * P], r)
+        def hidden_token_0(g):
+            f_planes[g] = work.tile([P, 4, P], BF16, name="f_planes")
+            for t in range(4):
                 nc.scalar.activation(
-                    out=f_grouped[g][:, r, :].rearrange("p (b u e) -> p b u e", u=2, e=2),
-                    in_=turned[:]
-                    .rearrange("p u b -> p (u b)")
-                    .bitcast(BF16)
-                    .rearrange("p (u b e) -> p b u e", u=2, e=2),
+                    out=f_planes[g][:, t, :],
+                    in_=x_psum[g][0][:, t, :],
                     func=AF.Relu,
+                    bias=bias[:, t : t + 1],
                 )
+
+        def hidden_tokens_1_2(g):
+            f_pre[g] = work.tile([P, 2, P, 4], BF16, name="f_pre")
+            nc.vector.scalar_tensor_tensor(
+                out=f_pre[g][:, 0],
+                in0=x_psum[g][1][:].rearrange("p t b -> p b t"),
+                scalar=-1.0,
+                in1=bias_grouped[:],
+                op0=ALU.mult,
+                op1=ALU.subtract,
+            )
+            nc.vector.tensor_tensor(
+                out=f_pre[g][:, 1],
+                in0=x_psum[g][2][:].rearrange("p t b -> p b t"),
+                in1=bias_grouped[:],
+                op=ALU.add,
+            )
+
+        def group_f(g):
+            f_grouped[g] = work.tile([P, R, 4 * P], BF16, name="f_grouped", align_bytes=64)
+            nc.vector.tensor_scalar_min(
+                out=f_grouped[g][:, 1, :],
+                in0=f_pre[g][:, 0].rearrange("p b t -> p (b t)"),
+                scalar1=0.0,
+            )
+            nc.vector.tensor_scalar_max(
+                out=f_grouped[g][:, 2, :],
+                in0=f_pre[g][:, 1].rearrange("p b t -> p (b t)"),
+                scalar1=0.0,
+            )
+            nc.vector.tensor_copy(
+                out=f_grouped[g][:, 0, :].rearrange("p (b t) -> p b t", t=4),
+                in_=f_planes[g][:].rearrange("p t b -> p b t"),
+            )
 
         def quantise_f(g):
             f_codes[g], f_scales[g] = quantise(f_grouped[g], "f")
 
         def second_matmul(g):
-            z1 = psum_turn.tile([P, H], F32, name="z1", tag="turn")
-            z0 = psum_z.tile([P, H], F32, name="z0", tag="z")
-            z2 = psum_z.tile([P, H], F32, name="z2", tag="z")
-            z_psum[g] = [z0, z1, z2]
-            for r in (1, 0, 2):
-                product(z_psum[g][r], f_codes[g], f_scales[g], r, w2_codes, w2_plane)
+            z0_minus_z1[g] = psum_z.tile([P, H], F32, name="z0_minus_z1")
+            z2_minus_z1[g] = psum_z.tile([P, H], F32, name="z2_minus_z1")
+            add_product(z0_minus_z1[g], g, 0, True)
+            add_product(z0_minus_z1[g], g, 1, False)
+            add_product(z2_minus_z1[g], g, 2, True)
+            add_product(z2_minus_z1[g], g, 1, False)
 
-        def copy_z1(g):
-            z1_sbuf[g] = work.tile([P, H], F32, name="z1_sbuf")
-            nc.scalar.copy(out=z1_sbuf[g][:], in_=z_psum[g][1][:])
-
-        def compare_logits(g):
-            z0, z2 = z_psum[g][0], z_psum[g][2]
-            larger = work.tile([P, H], F32, name="larger")
-            diff01[g] = work.tile([P, H], F32, name="diff01")
-            nc.vector.tensor_tensor(out=larger[:], in0=z0[:], in1=z1_sbuf[g][:], op=ALU.max)
-            nc.vector.tensor_tensor(out=diff01[g][:], in0=z0[:], in1=z1_sbuf[g][:], op=ALU.subtract)
-            nc.vector.tensor_tensor(out=logit2[g][:], in0=z2[:], in1=larger[:], op=ALU.subtract)
-
-        def first_tanh(g):
+        def compare_0_1(g):
+            relu01[g] = work.tile([P, H], F32, name="relu01")
             tanh1[g] = work.tile([P, H], F32, name="tanh1")
-            nc.scalar.activation(out=tanh1[g][:], in_=diff01[g][:], func=AF.Tanh, scale=0.5)
+            nc.scalar.activation(out=relu01[g][:], in_=z0_minus_z1[g][:], func=AF.Relu)
+            nc.scalar.activation(out=tanh1[g][:], in_=z0_minus_z1[g][:], func=AF.Tanh, scale=0.5)
+
+        def compare_2(g):
+            nc.vector.tensor_tensor(
+                out=logit2[g][:], in0=z2_minus_z1[g][:], in1=relu01[g][:], op=ALU.subtract
+            )
+
+        def absolute_tanh(g):
             nc.scalar.activation(out=abs_tanh[g][:], in_=tanh1[g][:], func=AF.Abs)
 
         def half_difference_0_1(g):
-            half_h0_minus_h1[g] = psum_z.tile([P, H], F32, name="half_h0_minus_h1", tag="z")
+            half_h0_minus_h1[g] = psum_z.tile([P, H], F32, name="half_h0_minus_h1")
             nc.tensor.matmul(
                 out=half_h0_minus_h1[g][:], lhsT=plus_half[:], rhs=h_sb[g][:, 0, :], start=True, stop=False
             )
@@ -221,18 +261,22 @@ def tile_blocksa_pa_t_kernel(
             if 0 <= g < N_GROUPS:
                 stage(g)
 
-        for t in range(-1, N_GROUPS + 3):
-            run(first_tanh, t - 2)
-            run(first_matmul, t)
-            run(quantise_f, t - 1)
+        for t in range(-3, N_GROUPS + 3):
             run(mix_tokens_0_and_1, t - 3)
-            run(second_matmul, t - 1)
-            run(copy_z1, t - 1)
             run(distance_to_token_2, t - 3)
             run(difference_2_1, t - 2)
-            run(turn_h, t + 1)
-            run(hidden_layer, t)
-            run(compare_logits, t - 1)
+            run(hidden_token_0, t)
+            run(hidden_tokens_1_2, t)
+            run(second_matmul, t - 2)
+            run(absolute_tanh, t - 3)
+            run(compare_0_1, t - 2)
+            run(compare_2, t - 2)
+            run(transpose_h, t + 3)
+            run(group_h, t + 3)
+            run(quantise_f, t - 1)
+            run(quantise_h, t + 2)
+            run(first_matmul, t + 1)
+            run(group_f, t)
             run(half_difference_0_1, t - 2)
 
         for g in range(N_GROUPS):

@@ -17,6 +17,8 @@ N_BLOCKS = 16 * 128
 N_GROUPS = N_BLOCKS // P
 WORDS = H // 2
 
+TOKEN_AT = (0, 2, 1)
+
 FLOPS = 2 * 2 * N_BLOCKS * R * H * H
 
 
@@ -46,7 +48,7 @@ def tile_blocksa_pa_t_kernel(
         tc.tile_pool(name="keep", bufs=1) as keep,
         tc.tile_pool(name="work", bufs=2) as work,
         tc.tile_pool(name="single", bufs=1) as single,
-        tc.psum_pool(name="psum_x", bufs=3) as psum_x,
+        tc.psum_pool(name="psum_x", bufs=1) as psum_x,
         tc.psum_pool(name="psum_z", bufs=1) as psum_z,
         tc.psum_pool(name="psum_turn", bufs=1) as psum_turn,
         tc.manual_schedule(),
@@ -90,18 +92,18 @@ def tile_blocksa_pa_t_kernel(
         logit2 = [keep.tile([P, H], F32, name="logit2_%d" % g) for g in range(N_GROUPS)]
         rest = [keep.tile([P, H], F32, name="rest%d" % g) for g in range(N_GROUPS)]
 
-        h_grouped, h_codes, h_scales, x_psum = {}, {}, {}, {}
-        turned_01, turned_2 = {}, {}
+        h_grouped, h_codes, h_scales = {}, {}, {}
+        turned_02, turned_1, x02_psum, x1_psum = {}, {}, {}, {}
         f_pre, f_planes, f_grouped, f_codes, f_scales = {}, {}, {}, {}, {}
         z0_minus_z1, z2_minus_z1 = {}, {}
         relu01, tanh1, half_h0_minus_h1, h2_minus_h1, mix = {}, {}, {}, {}, {}
 
         def transpose_h(g):
             h_words = h_sb[g][:].bitcast(F32)
-            turned_01[g] = psum_turn.tile([P, 2, 2, P], F32, name="turned_01")
-            turned_2[g] = psum_turn.tile([P, 2, P], F32, name="turned_2")
-            for r in range(R):
-                turned = turned_01[g][:, r] if r < 2 else turned_2[g][:]
+            turned_02[g] = psum_turn.tile([P, 2, 2, P], F32, name="turned_02")
+            turned_1[g] = psum_turn.tile([P, 2, P], F32, name="turned_1")
+            for place, r in enumerate(TOKEN_AT):
+                turned = turned_02[g][:, place] if place < 2 else turned_1[g][:]
                 for u in range(2):
                     nc.tensor.transpose(
                         out=turned[:, u, :], in_=h_words[:, r, u:WORDS:2], identity=ident[:]
@@ -111,11 +113,11 @@ def tile_blocksa_pa_t_kernel(
             h_grouped[g] = work.tile([P, R, 4 * P], BF16, name="h_grouped", align_bytes=64)
             nc.scalar.copy(
                 out=h_grouped[g][:, 0:2, :].bitcast(F32).rearrange("p r (b u) -> p r b u", u=2),
-                in_=turned_01[g][:].rearrange("p r u b -> p r b u"),
+                in_=turned_02[g][:].rearrange("p r u b -> p r b u"),
             )
             nc.scalar.copy(
                 out=h_grouped[g][:, 2, :].bitcast(F32).rearrange("p (b u) -> p b u", u=2),
-                in_=turned_2[g][:].rearrange("p u b -> p b u"),
+                in_=turned_1[g][:].rearrange("p u b -> p b u"),
             )
 
         def quantise(grouped, name):
@@ -128,11 +130,11 @@ def tile_blocksa_pa_t_kernel(
             return codes, scales
 
         def add_product(acc, g, r, start):
-            codes, scales = f_codes[g], f_scales[g]
+            place = TOKEN_AT.index(r)
             nc.tensor.matmul_mx(
                 out=acc[:],
-                lhsT=codes[:, r, :].bitcast(FP8X4),
-                lhsT_scale=scales[:, r, :],
+                lhsT=f_codes[g][:, place, :].bitcast(FP8X4),
+                lhsT_scale=f_scales[g][:, place, :],
                 rhs=w2_codes[:].bitcast(FP8X4),
                 rhs_scale=w2_plane[:],
                 start=start,
@@ -143,61 +145,54 @@ def tile_blocksa_pa_t_kernel(
             h_codes[g], h_scales[g] = quantise(h_grouped[g], "h")
 
         def first_matmul(g):
-            x_psum[g] = []
-            for r in range(R):
-                x_psum[g].append(psum_x.tile([P, 4, P], F32, name="x", tag="x"))
+            x02_psum[g] = [
+                psum_x.tile([P, 2, 2 * P], F32, name="x02_t01"),
+                psum_x.tile([P, 2, 2 * P], F32, name="x02_t23"),
+            ]
+            x1_psum[g] = psum_x.tile([P, 4, P], F32, name="x1")
+            for places, acc in (
+                (slice(0, 2), [x02_psum[g][t // 2][:, t % 2, :] for t in range(4)]),
+                (slice(2, 3), [x1_psum[g][:, t, :] for t in range(4)]),
+            ):
                 for t in range(4):
                     nc.tensor.matmul_mx(
-                        out=x_psum[g][r][:, t, :],
+                        out=acc[t],
                         lhsT=w1_turned[:, t * P : (t + 1) * P].bitcast(FP8X4),
                         lhsT_scale=w1_turned_plane[:, t * P : (t + 1) * P],
-                        rhs=h_codes[g][:, r, :].bitcast(FP8X4),
-                        rhs_scale=h_scales[g][:, r, :],
+                        rhs=h_codes[g][:, places, :].rearrange("p r b -> p (r b)").bitcast(FP8X4),
+                        rhs_scale=h_scales[g][:, places, :].rearrange("p r b -> p (r b)"),
                         start=True,
                         stop=True,
                     )
 
-        def hidden_token_0(g):
-            f_planes[g] = work.tile([P, 4, P], BF16, name="f_planes")
+        def hidden_tokens_0_2(g):
+            f_planes[g] = work.tile([P, 4, 2 * P], BF16, name="f_planes")
             for t in range(4):
                 nc.scalar.activation(
                     out=f_planes[g][:, t, :],
-                    in_=x_psum[g][0][:, t, :],
+                    in_=x02_psum[g][t // 2][:, t % 2, :],
                     func=AF.Relu,
                     bias=bias[:, t : t + 1],
                 )
 
-        def hidden_tokens_1_2(g):
-            f_pre[g] = work.tile([P, 2, P, 4], BF16, name="f_pre")
+        def hidden_token_1(g):
+            f_pre[g] = work.tile([P, P, 4], BF16, name="f_pre")
             nc.vector.scalar_tensor_tensor(
-                out=f_pre[g][:, 0],
-                in0=x_psum[g][1][:].rearrange("p t b -> p b t"),
+                out=f_pre[g][:],
+                in0=x1_psum[g][:].rearrange("p t b -> p b t"),
                 scalar=-1.0,
                 in1=bias_grouped[:],
                 op0=ALU.mult,
                 op1=ALU.subtract,
             )
-            nc.vector.tensor_tensor(
-                out=f_pre[g][:, 1],
-                in0=x_psum[g][2][:].rearrange("p t b -> p b t"),
-                in1=bias_grouped[:],
-                op=ALU.add,
-            )
 
         def group_f(g):
             f_grouped[g] = work.tile([P, R, 4 * P], BF16, name="f_grouped", align_bytes=64)
             nc.vector.tensor_scalar_min(
-                out=f_grouped[g][:, 1, :],
-                in0=f_pre[g][:, 0].rearrange("p b t -> p (b t)"),
-                scalar1=0.0,
-            )
-            nc.vector.tensor_scalar_max(
-                out=f_grouped[g][:, 2, :],
-                in0=f_pre[g][:, 1].rearrange("p b t -> p (b t)"),
-                scalar1=0.0,
+                out=f_grouped[g][:, 2, :], in0=f_pre[g][:].rearrange("p b t -> p (b t)"), scalar1=0.0
             )
             nc.vector.tensor_copy(
-                out=f_grouped[g][:, 0, :].rearrange("p (b t) -> p b t", t=4),
+                out=f_grouped[g][:, 0:2, :].rearrange("p r (b t) -> p (r b) t", t=4),
                 in_=f_planes[g][:].rearrange("p t b -> p b t"),
             )
 
@@ -247,7 +242,7 @@ def tile_blocksa_pa_t_kernel(
             )
 
         def distance_to_token_2(g):
-            nc.gpsimd.tensor_tensor(
+            nc.vector.tensor_tensor(
                 out=rest[g][:], in0=h2_minus_h1[g][:], in1=mix[g][:], op=ALU.subtract
             )
 
@@ -263,10 +258,9 @@ def tile_blocksa_pa_t_kernel(
 
         for t in range(-3, N_GROUPS + 3):
             run(mix_tokens_0_and_1, t - 3)
-            run(distance_to_token_2, t - 3)
-            run(difference_2_1, t - 2)
-            run(hidden_token_0, t)
-            run(hidden_tokens_1_2, t)
+            run(difference_2_1, t - 3)
+            run(hidden_tokens_0_2, t)
+            run(hidden_token_1, t)
             run(second_matmul, t - 2)
             run(absolute_tanh, t - 3)
             run(compare_0_1, t - 2)
@@ -276,6 +270,7 @@ def tile_blocksa_pa_t_kernel(
             run(quantise_f, t - 1)
             run(quantise_h, t + 2)
             run(first_matmul, t + 1)
+            run(distance_to_token_2, t - 3)
             run(group_f, t)
             run(half_difference_0_1, t - 2)
 

@@ -123,9 +123,11 @@ def tile_blocksa_pa_t_kernel(
         def quantise(grouped, name):
             codes = work.tile([P, R, P], U32, name=name + "_codes", align_bytes=64)
             scales = work.tile([P, R, P], U8, name=name + "_scales", align_bytes=64)
-            for r in range(R):
+            for places in (slice(0, 2), slice(2, 3)):
                 nc.vector.quantize_mx(
-                    out=codes[:, r, :].bitcast(FP8X4), scales=scales[:, r, :], in_=grouped[:, r, :]
+                    out=codes[:, places, :].rearrange("p r b -> p (r b)").bitcast(FP8X4),
+                    scales=scales[:, places, :].rearrange("p r b -> p (r b)"),
+                    in_=grouped[:, places, :].rearrange("p r k -> p (r k)"),
                 )
             return codes, scales
 
@@ -257,8 +259,8 @@ def tile_blocksa_pa_t_kernel(
                 stage(g)
 
         for t in range(-3, N_GROUPS + 3):
-            run(mix_tokens_0_and_1, t - 3)
             run(difference_2_1, t - 3)
+            run(mix_tokens_0_and_1, t - 3)
             run(hidden_tokens_0_2, t)
             run(hidden_token_1, t)
             run(second_matmul, t - 2)
@@ -270,8 +272,8 @@ def tile_blocksa_pa_t_kernel(
             run(quantise_f, t - 1)
             run(quantise_h, t + 2)
             run(first_matmul, t + 1)
-            run(distance_to_token_2, t - 3)
             run(group_f, t)
+            run(distance_to_token_2, t - 3)
             run(half_difference_0_1, t - 2)
 
         for g in range(N_GROUPS):

@@ -19,6 +19,8 @@ WORDS = H // 2
 
 TOKEN_AT = (0, 2, 1)
 
+EARLY = 6
+
 FLOPS = 2 * 2 * N_BLOCKS * R * H * H
 
 
@@ -94,6 +96,7 @@ def tile_blocksa_pa_t_kernel(
 
         h_grouped, h_codes, h_scales = {}, {}, {}
         turned_02, turned_1, x02_psum, x1_psum = {}, {}, {}, {}
+        planes1 = {}
         f_pre, f_planes, f_grouped, f_codes, f_scales = {}, {}, {}, {}, {}
         z0_minus_z1, z2_minus_z1 = {}, {}
         relu01, tanh1, half_h0_minus_h1, h2_minus_h1, mix = {}, {}, {}, {}, {}
@@ -178,6 +181,16 @@ def tile_blocksa_pa_t_kernel(
                 )
 
         def hidden_token_1(g):
+            if g >= 12:
+                planes1[g] = work.tile([P, 4, P], BF16, name="planes1")
+                for t in range(4):
+                    nc.scalar.activation(
+                        out=planes1[g][:, t, :],
+                        in_=x1_psum[g][:, t, :],
+                        func=AF.Relu,
+                        bias=bias[:, t : t + 1],
+                    )
+                return
             f_pre[g] = work.tile([P, P, 4], BF16, name="f_pre")
             nc.vector.scalar_tensor_tensor(
                 out=f_pre[g][:],
@@ -190,12 +203,21 @@ def tile_blocksa_pa_t_kernel(
 
         def group_f(g):
             f_grouped[g] = work.tile([P, R, 4 * P], BF16, name="f_grouped", align_bytes=64)
-            nc.vector.tensor_scalar_min(
-                out=f_grouped[g][:, 2, :], in0=f_pre[g][:].rearrange("p b t -> p (b t)"), scalar1=0.0
-            )
+            if g >= 12:
+                nc.vector.tensor_scalar_mul(
+                    out=f_grouped[g][:, 2, :].rearrange("p (c i t) -> p c t i", i=4, t=4),
+                    in0=planes1[g][:].rearrange("p t (c i) -> p c t i", i=4),
+                    scalar1=-1.0,
+                )
+            else:
+                nc.vector.tensor_scalar_min(
+                    out=f_grouped[g][:, 2, :],
+                    in0=f_pre[g][:].rearrange("p b t -> p (b t)"),
+                    scalar1=0.0,
+                )
             nc.vector.tensor_copy(
-                out=f_grouped[g][:, 0:2, :].rearrange("p r (b t) -> p (r b) t", t=4),
-                in_=f_planes[g][:].rearrange("p t b -> p b t"),
+                out=f_grouped[g][:, 0:2, :].rearrange("p r (c i t) -> p (r c) t i", i=4, t=4),
+                in_=f_planes[g][:].rearrange("p t (c i) -> p c t i", i=4),
             )
 
         def quantise_f(g):
@@ -254,11 +276,35 @@ def tile_blocksa_pa_t_kernel(
                 out=h2_minus_h1[g][:], in0=h_sb[g][:, 2, :], in1=h_sb[g][:, 1, :], op=ALU.subtract
             )
 
+        def logarithm(g):
+            nc.scalar.activation(
+                out=abs_tanh[g][:], in_=abs_tanh[g][:], func=AF.Ln, scale=0.5, bias=half[:]
+            )
+
+        def combine(g):
+            nc.vector.tensor_tensor(
+                out=logit2[g][:], in0=logit2[g][:], in1=abs_tanh[g][:], op=ALU.add
+            )
+
+        def second_tanh(g):
+            nc.scalar.activation(out=logit2[g][:], in_=logit2[g][:], func=AF.Tanh, scale=0.5)
+
+        def weigh(g):
+            nc.vector.scalar_tensor_tensor(
+                out=rest[g][:], in0=logit2[g][:], scalar=-1.0, in1=rest[g][:], op0=ALU.add, op1=ALU.mult
+            )
+
+        def store(g):
+            nc.vector.scalar_tensor_tensor(
+                out=rest[g][:], in0=rest[g][:], scalar=0.5, in1=h_sb[g][:, 2, :], op0=ALU.mult, op1=ALU.add
+            )
+            nc.sync.dma_start(out=out_groups[:, g, :], in_=rest[g][:])
+
         def run(stage, g):
             if 0 <= g < N_GROUPS:
                 stage(g)
 
-        for t in range(-3, N_GROUPS + 3):
+        for t in range(-3, N_GROUPS + 1):
             run(difference_2_1, t - 3)
             run(mix_tokens_0_and_1, t - 3)
             run(hidden_tokens_0_2, t)
@@ -276,32 +322,37 @@ def tile_blocksa_pa_t_kernel(
             run(distance_to_token_2, t - 3)
             run(half_difference_0_1, t - 2)
 
-        for g in range(N_GROUPS):
-            nc.scalar.activation(
-                out=abs_tanh[g][:], in_=abs_tanh[g][:], func=AF.Ln, scale=0.5, bias=half[:]
-            )
-        for g in range(N_GROUPS):
-            nc.vector.tensor_tensor(
-                out=logit2[g][:], in0=logit2[g][:], in1=abs_tanh[g][:], op=ALU.add
-            )
-            nc.scalar.activation(out=logit2[g][:], in_=logit2[g][:], func=AF.Tanh, scale=0.5)
-        for g in range(N_GROUPS + 1):
+        last = N_GROUPS - 1
+        difference_2_1(last - 1)
+        mix_tokens_0_and_1(last - 1)
+        second_matmul(last)
+        absolute_tanh(last - 1)
+        distance_to_token_2(last - 1)
+        half_difference_0_1(last)
+        for g in range(EARLY):
+            logarithm(g)
+            combine(g)
+        compare_0_1(last)
+        compare_2(last)
+        difference_2_1(last)
+        mix_tokens_0_and_1(last)
+        for g in range(EARLY):
+            second_tanh(g)
+        absolute_tanh(last)
+        for g in range(EARLY, N_GROUPS):
+            logarithm(g)
+        distance_to_token_2(last)
+        for g in range(EARLY + 1):
+            if g < EARLY:
+                weigh(g)
+            if g > 0:
+                store(g - 1)
+        for g in range(EARLY, N_GROUPS):
+            combine(g)
+        for g in range(EARLY, N_GROUPS):
+            second_tanh(g)
+        for g in range(EARLY, N_GROUPS + 1):
             if g < N_GROUPS:
-                nc.vector.scalar_tensor_tensor(
-                    out=rest[g][:],
-                    in0=logit2[g][:],
-                    scalar=-1.0,
-                    in1=rest[g][:],
-                    op0=ALU.add,
-                    op1=ALU.mult,
-                )
-            if g >= 1:
-                nc.vector.scalar_tensor_tensor(
-                    out=rest[g - 1][:],
-                    in0=rest[g - 1][:],
-                    scalar=0.5,
-                    in1=h_sb[g - 1][:, 2, :],
-                    op0=ALU.mult,
-                    op1=ALU.add,
-                )
-                nc.sync.dma_start(out=out_groups[:, g - 1, :], in_=rest[g - 1][:])
+                weigh(g)
+            if g > EARLY:
+                store(g - 1)

@@ -21,6 +21,10 @@ TOKEN_AT = (0, 2, 1)
 
 EARLY = 6
 
+H_AHEAD = 3
+
+WITHOUT_PSUM_TIME = (0, N_GROUPS - 2, N_GROUPS - 1)
+
 FLOPS = 2 * 2 * N_BLOCKS * R * H * H
 
 
@@ -55,12 +59,14 @@ def tile_blocksa_pa_t_kernel(
         tc.psum_pool(name="psum_turn", bufs=1) as psum_turn,
         tc.manual_schedule(),
     ):
-        h_sb = [keep.tile([P, R, H], BF16, name="h%d" % g) for g in range(N_GROUPS)]
+        h_all = keep.tile([P, N_GROUPS, R, H], BF16, name="h_all")
+        h_sb = [h_all[:, g] for g in range(N_GROUPS)]
         nc.sync.dma_start(out=h_sb[0][:], in_=h_groups[:, 0])
-        w1_codes, w1_plane = load_weight(nc, keep, s2t_W1_w_words, s2t_W1_w_scales, "w1")
         nc.sync.dma_start(out=h_sb[1][:], in_=h_groups[:, 1])
+        w1_codes, w1_plane = load_weight(nc, keep, s2t_W1_w_words, s2t_W1_w_scales, "w1")
+        nc.sync.dma_start(out=h_sb[2][:], in_=h_groups[:, 2])
         w2_codes, w2_plane = load_weight(nc, keep, s2t_W_w_words, s2t_W_w_scales, "w2")
-        for g in range(2, N_GROUPS):
+        for g in range(3, N_GROUPS):
             nc.sync.dma_start(out=h_sb[g][:], in_=h_groups[:, g])
 
         bias_bf16 = keep.tile([P, 4], BF16, name="bias_bf16")
@@ -90,14 +96,17 @@ def tile_blocksa_pa_t_kernel(
             in_=w1_plane[:].rearrange("p (m t) -> p m t", t=4),
         )
 
-        abs_tanh = [keep.tile([P, H], F32, name="abs_tanh%d" % g) for g in range(N_GROUPS)]
-        logit2 = [keep.tile([P, H], F32, name="logit2_%d" % g) for g in range(N_GROUPS)]
-        rest = [keep.tile([P, H], F32, name="rest%d" % g) for g in range(N_GROUPS)]
+        abs_tanh_all = keep.tile([P, N_GROUPS, H], F32, name="abs_tanh_all")
+        logit2_all = keep.tile([P, N_GROUPS, H], F32, name="logit2_all")
+        rest_all = keep.tile([P, N_GROUPS, H], F32, name="rest_all")
+        abs_tanh = [abs_tanh_all[:, g] for g in range(N_GROUPS)]
+        logit2 = [logit2_all[:, g] for g in range(N_GROUPS)]
+        rest = [rest_all[:, g] for g in range(N_GROUPS)]
 
-        h_grouped, h_codes, h_scales = {}, {}, {}
+        grouped, codes, scales = {}, {}, {}
         turned_02, turned_1, x02_psum, x1_psum = {}, {}, {}, {}
         planes1 = {}
-        f_pre, f_planes, f_grouped, f_codes, f_scales = {}, {}, {}, {}, {}
+        f_pre, f_planes = {}, {}
         z0_minus_z1, z2_minus_z1 = {}, {}
         relu01, tanh1, half_h0_minus_h1, h2_minus_h1, mix = {}, {}, {}, {}, {}
 
@@ -113,43 +122,51 @@ def tile_blocksa_pa_t_kernel(
                     )
 
         def group_h(g):
-            h_grouped[g] = work.tile([P, R, 4 * P], BF16, name="h_grouped", align_bytes=64)
+            h_grouped = grouped[g - H_AHEAD][:, R:, :]
             nc.scalar.copy(
-                out=h_grouped[g][:, 0:2, :].bitcast(F32).rearrange("p r (b u) -> p r b u", u=2),
+                out=h_grouped[:, 0:2, :].bitcast(F32).rearrange("p r (b u) -> p r b u", u=2),
                 in_=turned_02[g][:].rearrange("p r u b -> p r b u"),
             )
             nc.scalar.copy(
-                out=h_grouped[g][:, 2, :].bitcast(F32).rearrange("p (b u) -> p b u", u=2),
+                out=h_grouped[:, 2, :].bitcast(F32).rearrange("p (b u) -> p b u", u=2),
                 in_=turned_1[g][:].rearrange("p u b -> p b u"),
             )
 
-        def quantise(grouped, name):
-            codes = work.tile([P, R, P], U32, name=name + "_codes", align_bytes=64)
-            scales = work.tile([P, R, P], U8, name=name + "_scales", align_bytes=64)
-            for places in (slice(0, 2), slice(2, 3)):
+        def open_turn(t):
+            grouped[t] = work.tile([P, 2 * R, 4 * P], BF16, name="grouped", align_bytes=64)
+
+        def quantise(t):
+            codes[t] = work.tile([P, 2 * R, P], U32, name="codes", align_bytes=64)
+            scales[t] = work.tile([P, 2 * R, P], U8, name="scales", align_bytes=64)
+            if t < 0:
+                parts = ((R, 2), (R + 2, 1))
+            elif t + H_AHEAD < N_GROUPS:
+                parts = ((0, 4), (4, 2))
+            else:
+                parts = ((0, 2), (2, 1))
+            for first, count in parts:
+                tokens = slice(first, first + count)
                 nc.vector.quantize_mx(
-                    out=codes[:, places, :].rearrange("p r b -> p (r b)").bitcast(FP8X4),
-                    scales=scales[:, places, :].rearrange("p r b -> p (r b)"),
-                    in_=grouped[:, places, :].rearrange("p r k -> p (r k)"),
+                    out=codes[t][:, tokens, :].rearrange("p r b -> p (r b)").bitcast(FP8X4),
+                    scales=scales[t][:, tokens, :].rearrange("p r b -> p (r b)"),
+                    in_=grouped[t][:, tokens, :].rearrange("p r k -> p (r k)"),
                 )
-            return codes, scales
 
         def add_product(acc, g, r, start):
             place = TOKEN_AT.index(r)
             nc.tensor.matmul_mx(
                 out=acc[:],
-                lhsT=f_codes[g][:, place, :].bitcast(FP8X4),
-                lhsT_scale=f_scales[g][:, place, :],
+                lhsT=codes[g][:, place, :].bitcast(FP8X4),
+                lhsT_scale=scales[g][:, place, :],
                 rhs=w2_codes[:].bitcast(FP8X4),
                 rhs_scale=w2_plane[:],
                 start=start,
                 stop=not start,
             )
 
-        def quantise_h(g):
-            h_codes[g], h_scales[g] = quantise(h_grouped[g], "h")
-
         def first_matmul(g):
+            h_codes = codes[g - H_AHEAD][:, R:, :]
+            h_scales = scales[g - H_AHEAD][:, R:, :]
             x02_psum[g] = [
                 psum_x.tile([P, 2, 2 * P], F32, name="x02_t01"),
                 psum_x.tile([P, 2, 2 * P], F32, name="x02_t23"),
@@ -164,8 +181,8 @@ def tile_blocksa_pa_t_kernel(
                         out=acc[t],
                         lhsT=w1_turned[:, t * P : (t + 1) * P].bitcast(FP8X4),
                         lhsT_scale=w1_turned_plane[:, t * P : (t + 1) * P],
-                        rhs=h_codes[g][:, places, :].rearrange("p r b -> p (r b)").bitcast(FP8X4),
-                        rhs_scale=h_scales[g][:, places, :].rearrange("p r b -> p (r b)"),
+                        rhs=h_codes[:, places, :].rearrange("p r b -> p (r b)").bitcast(FP8X4),
+                        rhs_scale=h_scales[:, places, :].rearrange("p r b -> p (r b)"),
                         start=True,
                         stop=True,
                     )
@@ -181,7 +198,7 @@ def tile_blocksa_pa_t_kernel(
                 )
 
         def hidden_token_1(g):
-            if g >= 12:
+            if g >= 13:
                 planes1[g] = work.tile([P, 4, P], BF16, name="planes1")
                 for t in range(4):
                     nc.scalar.activation(
@@ -202,26 +219,23 @@ def tile_blocksa_pa_t_kernel(
             )
 
         def group_f(g):
-            f_grouped[g] = work.tile([P, R, 4 * P], BF16, name="f_grouped", align_bytes=64)
-            if g >= 12:
+            f_grouped = grouped[g][:, 0:R, :]
+            if g >= 13:
                 nc.vector.tensor_scalar_mul(
-                    out=f_grouped[g][:, 2, :].rearrange("p (c i t) -> p c t i", i=4, t=4),
+                    out=f_grouped[:, 2, :].rearrange("p (c i t) -> p c t i", i=4, t=4),
                     in0=planes1[g][:].rearrange("p t (c i) -> p c t i", i=4),
                     scalar1=-1.0,
                 )
             else:
                 nc.vector.tensor_scalar_min(
-                    out=f_grouped[g][:, 2, :],
+                    out=f_grouped[:, 2, :],
                     in0=f_pre[g][:].rearrange("p b t -> p (b t)"),
                     scalar1=0.0,
                 )
             nc.vector.tensor_copy(
-                out=f_grouped[g][:, 0:2, :].rearrange("p r (c i t) -> p (r c) t i", i=4, t=4),
+                out=f_grouped[:, 0:2, :].rearrange("p r (c i t) -> p (r c) t i", i=4, t=4),
                 in_=f_planes[g][:].rearrange("p t (c i) -> p c t i", i=4),
             )
-
-        def quantise_f(g):
-            f_codes[g], f_scales[g] = quantise(f_grouped[g], "f")
 
         def second_matmul(g):
             z0_minus_z1[g] = psum_z.tile([P, H], F32, name="z0_minus_z1")
@@ -272,40 +286,70 @@ def tile_blocksa_pa_t_kernel(
 
         def difference_2_1(g):
             h2_minus_h1[g] = single.tile([P, H], F32, name="h2_minus_h1")
-            nc.gpsimd.tensor_tensor(
+            engine = nc.vector if g in WITHOUT_PSUM_TIME else nc.gpsimd
+            engine.tensor_tensor(
                 out=h2_minus_h1[g][:], in0=h_sb[g][:, 2, :], in1=h_sb[g][:, 1, :], op=ALU.subtract
             )
 
-        def logarithm(g):
+        def logarithm(groups):
             nc.scalar.activation(
-                out=abs_tanh[g][:], in_=abs_tanh[g][:], func=AF.Ln, scale=0.5, bias=half[:]
+                out=abs_tanh_all[:, groups],
+                in_=abs_tanh_all[:, groups],
+                func=AF.Ln,
+                scale=0.5,
+                bias=half[:],
             )
 
-        def combine(g):
+        def combine(groups):
             nc.vector.tensor_tensor(
-                out=logit2[g][:], in0=logit2[g][:], in1=abs_tanh[g][:], op=ALU.add
+                out=logit2_all[:, groups],
+                in0=logit2_all[:, groups],
+                in1=abs_tanh_all[:, groups],
+                op=ALU.add,
             )
 
-        def second_tanh(g):
-            nc.scalar.activation(out=logit2[g][:], in_=logit2[g][:], func=AF.Tanh, scale=0.5)
+        def second_tanh(groups):
+            nc.scalar.activation(
+                out=logit2_all[:, groups], in_=logit2_all[:, groups], func=AF.Tanh, scale=0.5
+            )
 
-        def weigh(g):
+        def weigh(groups, columns):
             nc.vector.scalar_tensor_tensor(
-                out=rest[g][:], in0=logit2[g][:], scalar=-1.0, in1=rest[g][:], op0=ALU.add, op1=ALU.mult
+                out=rest_all[:, groups, columns],
+                in0=logit2_all[:, groups, columns],
+                scalar=-1.0,
+                in1=rest_all[:, groups, columns],
+                op0=ALU.add,
+                op1=ALU.mult,
             )
 
-        def store(g):
+        def store(groups, columns):
             nc.vector.scalar_tensor_tensor(
-                out=rest[g][:], in0=rest[g][:], scalar=0.5, in1=h_sb[g][:, 2, :], op0=ALU.mult, op1=ALU.add
+                out=rest_all[:, groups, columns],
+                in0=rest_all[:, groups, columns],
+                scalar=0.5,
+                in1=h_all[:, groups, 2, columns],
+                op0=ALU.mult,
+                op1=ALU.add,
             )
-            nc.sync.dma_start(out=out_groups[:, g, :], in_=rest[g][:])
+            nc.sync.dma_start(
+                out=out_groups[:, groups, columns], in_=rest_all[:, groups, columns]
+            )
+
+        def finish(pieces):
+            for piece, before in zip(pieces + [None], [None] + pieces):
+                if piece:
+                    weigh(*piece)
+                if before:
+                    store(*before)
 
         def run(stage, g):
             if 0 <= g < N_GROUPS:
                 stage(g)
 
-        for t in range(-3, N_GROUPS + 1):
-            run(difference_2_1, t - 3)
+        for t in range(-H_AHEAD, N_GROUPS + 1):
+            if t > H_AHEAD:
+                run(difference_2_1, t - 3)
             run(mix_tokens_0_and_1, t - 3)
             run(hidden_tokens_0_2, t)
             run(hidden_token_1, t)
@@ -313,15 +357,22 @@ def tile_blocksa_pa_t_kernel(
             run(absolute_tanh, t - 3)
             run(compare_0_1, t - 2)
             run(compare_2, t - 2)
-            run(transpose_h, t + 3)
-            run(group_h, t + 3)
-            run(quantise_f, t - 1)
-            run(quantise_h, t + 2)
+            run(transpose_h, t + H_AHEAD)
+            if t < N_GROUPS:
+                open_turn(t)
+            run(group_h, t + H_AHEAD)
+            if t > -H_AHEAD:
+                quantise(t - 1)
             run(first_matmul, t + 1)
+            if t == -1:
+                difference_2_1(0)
             run(group_f, t)
             run(distance_to_token_2, t - 3)
             run(half_difference_0_1, t - 2)
 
+        all_columns = slice(0, H)
+        early = [slice(g, g + 2) for g in range(0, EARLY, 2)]
+        late = [slice(g, g + 2) for g in range(EARLY, N_GROUPS, 2)]
         last = N_GROUPS - 1
         difference_2_1(last - 1)
         mix_tokens_0_and_1(last - 1)
@@ -329,30 +380,27 @@ def tile_blocksa_pa_t_kernel(
         absolute_tanh(last - 1)
         distance_to_token_2(last - 1)
         half_difference_0_1(last)
-        for g in range(EARLY):
-            logarithm(g)
-            combine(g)
+        for groups in early:
+            logarithm(groups)
+            combine(groups)
         compare_0_1(last)
         compare_2(last)
         difference_2_1(last)
         mix_tokens_0_and_1(last)
-        for g in range(EARLY):
-            second_tanh(g)
+        for groups in early:
+            second_tanh(groups)
         absolute_tanh(last)
-        for g in range(EARLY, N_GROUPS):
-            logarithm(g)
+        for groups in late:
+            logarithm(groups)
         distance_to_token_2(last)
-        for g in range(EARLY + 1):
-            if g < EARLY:
-                weigh(g)
-            if g > 0:
-                store(g - 1)
-        for g in range(EARLY, N_GROUPS):
-            combine(g)
-        for g in range(EARLY, N_GROUPS):
-            second_tanh(g)
-        for g in range(EARLY, N_GROUPS + 1):
-            if g < N_GROUPS:
-                weigh(g)
-            if g > EARLY:
-                store(g - 1)
+        finish([(groups, all_columns) for groups in early])
+        for groups in late:
+            combine(groups)
+        one_by_one = [slice(EARLY, EARLY + 1), slice(EARLY + 1, EARLY + 2)]
+        for groups in one_by_one + late[1:]:
+            second_tanh(groups)
+        finish(
+            [(groups, all_columns) for groups in one_by_one + late[1:-1]]
+            + [(slice(last - 1, last), all_columns)]
+            + [(slice(last, last + 1), slice(0, H // 2)), (slice(last, last + 1), slice(H // 2, H))]
+        )

import concourse.mybir as mybir
from concourse.masks import make_identity

F32 = mybir.dt.float32
BF16 = mybir.dt.bfloat16
I32 = mybir.dt.int32
U32 = mybir.dt.uint32
U8 = mybir.dt.uint8
FP8X4 = mybir.dt.float8_e4m3fn_x4
AF = mybir.ActivationFunctionType
ALU = mybir.AluOpType

P = 128
H = 512
R = 3
N_BLOCKS = 16 * 128
N_GROUPS = N_BLOCKS // P
WORDS = H // 2

TOKEN_AT = (0, 2, 1)

EARLY = 6

H_AHEAD = 3

WITHOUT_PSUM_TIME = (0, N_GROUPS - 2, N_GROUPS - 1)

FLOPS = 2 * 2 * N_BLOCKS * R * H * H


def load_weight(nc, pool, words, scales, name):
    codes = pool.tile([P, H], U32, name=name + "_codes", align_bytes=64)
    plane = pool.tile([P, H], U8, name=name + "_plane", align_bytes=64)
    nc.vector.memset(plane[:].bitcast(I32), 0)
    nc.sync.dma_start(
        out=codes[:].bitcast(I32), in_=words[0].rearrange("p n t -> p (n t)").bitcast(I32)
    )
    for quadrant in range(4):
        nc.sync.dma_start(
            out=plane[32 * quadrant : 32 * quadrant + 4, :].bitcast(I32),
            in_=scales[0, 4 * quadrant : 4 * quadrant + 4, :].bitcast(I32),
        )
    return codes, plane


def tile_blocksa_pa_t_kernel(
    tc, h, s2t_W1_w_words, s2t_W1_w_scales, s2t_W1_b, s2t_W_w_words, s2t_W_w_scales, out
):
    nc = tc.nc
    h_groups = h.rearrange("b n r c -> (b n) r c").rearrange("(p g) r c -> p g r c", g=N_GROUPS)
    out_groups = out.rearrange("b n c -> (b n) c").rearrange("(p g) c -> p g c", g=N_GROUPS)

    with (
        tc.tile_pool(name="keep", bufs=1) as keep,
        tc.tile_pool(name="work", bufs=2) as work,
        tc.tile_pool(name="single", bufs=1) as single,
        tc.psum_pool(name="psum_x", bufs=1) as psum_x,
        tc.psum_pool(name="psum_z", bufs=1) as psum_z,
        tc.psum_pool(name="psum_turn", bufs=1) as psum_turn,
        tc.manual_schedule(),
    ):
        h_all = keep.tile([P, N_GROUPS, R, H], BF16, name="h_all")
        h_sb = [h_all[:, g] for g in range(N_GROUPS)]
        nc.sync.dma_start(out=h_sb[0][:], in_=h_groups[:, 0])
        nc.sync.dma_start(out=h_sb[1][:], in_=h_groups[:, 1])
        w1_codes, w1_plane = load_weight(nc, keep, s2t_W1_w_words, s2t_W1_w_scales, "w1")
        nc.sync.dma_start(out=h_sb[2][:], in_=h_groups[:, 2])
        w2_codes, w2_plane = load_weight(nc, keep, s2t_W_w_words, s2t_W_w_scales, "w2")
        for g in range(3, N_GROUPS):
            nc.sync.dma_start(out=h_sb[g][:], in_=h_groups[:, g])

        bias_bf16 = keep.tile([P, 4], BF16, name="bias_bf16")
        nc.scalar.dma_start(out=bias_bf16[:], in_=s2t_W1_b.rearrange("(p t) -> p t", t=4))
        bias = keep.tile([P, 4], F32, name="bias")
        nc.vector.tensor_copy(out=bias[:], in_=bias_bf16[:])
        bias_grouped = keep.tile([P, P, 4], F32, name="bias_grouped")
        nc.vector.tensor_copy(out=bias_grouped[:], in_=bias[:].unsqueeze(1).to_broadcast([P, P, 4]))

        half = keep.tile([P, 1], F32, name="half")
        nc.vector.memset(half[:], 0.5)
        ident = keep.tile([P, P], F32, name="ident")
        make_identity(nc, ident[:])
        plus_half = keep.tile([P, P], BF16, name="plus_half")
        minus_half = keep.tile([P, P], BF16, name="minus_half")
        nc.vector.tensor_scalar_mul(out=plus_half[:], in0=ident[:], scalar1=0.5)
        nc.vector.tensor_scalar_mul(out=minus_half[:], in0=ident[:], scalar1=-0.5)

        w1_turned = keep.tile([P, H], U32, name="w1_turned", align_bytes=64)
        w1_turned_plane = keep.tile([P, H], U8, name="w1_turned_plane", align_bytes=64)
        nc.vector.tensor_copy(
            out=w1_turned[:].bitcast(I32).rearrange("p (t m) -> p t m", t=4),
            in_=w1_codes[:].bitcast(I32).rearrange("p (m t) -> p t m", t=4),
        )
        nc.vector.tensor_copy(
            out=w1_turned_plane[:].rearrange("p (t m) -> p m t", t=4),
            in_=w1_plane[:].rearrange("p (m t) -> p m t", t=4),
        )

        abs_tanh_all = keep.tile([P, N_GROUPS, H], F32, name="abs_tanh_all")
        logit2_all = keep.tile([P, N_GROUPS, H], F32, name="logit2_all")
        rest_all = keep.tile([P, N_GROUPS, H], F32, name="rest_all")
        abs_tanh = [abs_tanh_all[:, g] for g in range(N_GROUPS)]
        logit2 = [logit2_all[:, g] for g in range(N_GROUPS)]
        rest = [rest_all[:, g] for g in range(N_GROUPS)]

        grouped, codes, scales = {}, {}, {}
        turned_02, turned_1, x02_psum, x1_psum = {}, {}, {}, {}
        planes1 = {}
        f_pre, f_planes = {}, {}
        z0_minus_z1, z2_minus_z1 = {}, {}
        relu01, tanh1, half_h0_minus_h1, h2_minus_h1, mix = {}, {}, {}, {}, {}

        def transpose_h(g):
            h_words = h_sb[g][:].bitcast(F32)
            turned_02[g] = psum_turn.tile([P, 2, 2, P], F32, name="turned_02")
            turned_1[g] = psum_turn.tile([P, 2, P], F32, name="turned_1")
            for place, r in enumerate(TOKEN_AT):
                turned = turned_02[g][:, place] if place < 2 else turned_1[g][:]
                for u in range(2):
                    nc.tensor.transpose(
                        out=turned[:, u, :], in_=h_words[:, r, u:WORDS:2], identity=ident[:]
                    )

        def group_h(g):
            h_grouped = grouped[g - H_AHEAD][:, R:, :]
            nc.scalar.copy(
                out=h_grouped[:, 0:2, :].bitcast(F32).rearrange("p r (b u) -> p r b u", u=2),
                in_=turned_02[g][:].rearrange("p r u b -> p r b u"),
            )
            nc.scalar.copy(
                out=h_grouped[:, 2, :].bitcast(F32).rearrange("p (b u) -> p b u", u=2),
                in_=turned_1[g][:].rearrange("p u b -> p b u"),
            )

        def open_turn(t):
            grouped[t] = work.tile([P, 2 * R, 4 * P], BF16, name="grouped", align_bytes=64)

        def quantise(t):
            codes[t] = work.tile([P, 2 * R, P], U32, name="codes", align_bytes=64)
            scales[t] = work.tile([P, 2 * R, P], U8, name="scales", align_bytes=64)
            if t < 0:
                parts = ((R, 2), (R + 2, 1))
            elif t + H_AHEAD < N_GROUPS:
                parts = ((0, 4), (4, 2))
            else:
                parts = ((0, 2), (2, 1))
            for first, count in parts:
                tokens = slice(first, first + count)
                nc.vector.quantize_mx(
                    out=codes[t][:, tokens, :].rearrange("p r b -> p (r b)").bitcast(FP8X4),
                    scales=scales[t][:, tokens, :].rearrange("p r b -> p (r b)"),
                    in_=grouped[t][:, tokens, :].rearrange("p r k -> p (r k)"),
                )

        def add_product(acc, g, r, start):
            place = TOKEN_AT.index(r)
            nc.tensor.matmul_mx(
                out=acc[:],
                lhsT=codes[g][:, place, :].bitcast(FP8X4),
                lhsT_scale=scales[g][:, place, :],
                rhs=w2_codes[:].bitcast(FP8X4),
                rhs_scale=w2_plane[:],
                start=start,
                stop=not start,
            )

        def first_matmul(g):
            h_codes = codes[g - H_AHEAD][:, R:, :]
            h_scales = scales[g - H_AHEAD][:, R:, :]
            x02_psum[g] = [
                psum_x.tile([P, 2, 2 * P], F32, name="x02_t01"),
                psum_x.tile([P, 2, 2 * P], F32, name="x02_t23"),
            ]
            x1_psum[g] = psum_x.tile([P, 4, P], F32, name="x1")
            for places, acc in (
                (slice(0, 2), [x02_psum[g][t // 2][:, t % 2, :] for t in range(4)]),
                (slice(2, 3), [x1_psum[g][:, t, :] for t in range(4)]),
            ):
                for t in range(4):
                    nc.tensor.matmul_mx(
                        out=acc[t],
                        lhsT=w1_turned[:, t * P : (t + 1) * P].bitcast(FP8X4),
                        lhsT_scale=w1_turned_plane[:, t * P : (t + 1) * P],
                        rhs=h_codes[:, places, :].rearrange("p r b -> p (r b)").bitcast(FP8X4),
                        rhs_scale=h_scales[:, places, :].rearrange("p r b -> p (r b)"),
                        start=True,
                        stop=True,
                    )

        def hidden_tokens_0_2(g):
            f_planes[g] = work.tile([P, 4, 2 * P], BF16, name="f_planes")
            for t in range(4):
                nc.scalar.activation(
                    out=f_planes[g][:, t, :],
                    in_=x02_psum[g][t // 2][:, t % 2, :],
                    func=AF.Relu,
                    bias=bias[:, t : t + 1],
                )

        def hidden_token_1(g):
            if g >= 13:
                planes1[g] = work.tile([P, 4, P], BF16, name="planes1")
                for t in range(4):
                    nc.scalar.activation(
                        out=planes1[g][:, t, :],
                        in_=x1_psum[g][:, t, :],
                        func=AF.Relu,
                        bias=bias[:, t : t + 1],
                    )
                return
            f_pre[g] = work.tile([P, P, 4], BF16, name="f_pre")
            nc.vector.scalar_tensor_tensor(
                out=f_pre[g][:],
                in0=x1_psum[g][:].rearrange("p t b -> p b t"),
                scalar=-1.0,
                in1=bias_grouped[:],
                op0=ALU.mult,
                op1=ALU.subtract,
            )

        def group_f(g):
            f_grouped = grouped[g][:, 0:R, :]
            if g >= 13:
                nc.vector.tensor_scalar_mul(
                    out=f_grouped[:, 2, :].rearrange("p (c i t) -> p c t i", i=4, t=4),
                    in0=planes1[g][:].rearrange("p t (c i) -> p c t i", i=4),
                    scalar1=-1.0,
                )
            else:
                nc.vector.tensor_scalar_min(
                    out=f_grouped[:, 2, :],
                    in0=f_pre[g][:].rearrange("p b t -> p (b t)"),
                    scalar1=0.0,
                )
            nc.vector.tensor_copy(
                out=f_grouped[:, 0:2, :].rearrange("p r (c i t) -> p (r c) t i", i=4, t=4),
                in_=f_planes[g][:].rearrange("p t (c i) -> p c t i", i=4),
            )

        def second_matmul(g):
            z0_minus_z1[g] = psum_z.tile([P, H], F32, name="z0_minus_z1")
            z2_minus_z1[g] = psum_z.tile([P, H], F32, name="z2_minus_z1")
            add_product(z0_minus_z1[g], g, 0, True)
            add_product(z0_minus_z1[g], g, 1, False)
            add_product(z2_minus_z1[g], g, 2, True)
            add_product(z2_minus_z1[g], g, 1, False)

        def compare_0_1(g):
            relu01[g] = work.tile([P, H], F32, name="relu01")
            tanh1[g] = work.tile([P, H], F32, name="tanh1")
            nc.scalar.activation(out=relu01[g][:], in_=z0_minus_z1[g][:], func=AF.Relu)
            nc.scalar.activation(out=tanh1[g][:], in_=z0_minus_z1[g][:], func=AF.Tanh, scale=0.5)

        def compare_2(g):
            nc.vector.tensor_tensor(
                out=logit2[g][:], in0=z2_minus_z1[g][:], in1=relu01[g][:], op=ALU.subtract
            )

        def absolute_tanh(g):
            nc.scalar.activation(out=abs_tanh[g][:], in_=tanh1[g][:], func=AF.Abs)

        def half_difference_0_1(g):
            half_h0_minus_h1[g] = psum_z.tile([P, H], F32, name="half_h0_minus_h1")
            nc.tensor.matmul(
                out=half_h0_minus_h1[g][:], lhsT=plus_half[:], rhs=h_sb[g][:, 0, :], start=True, stop=False
            )
            nc.tensor.matmul(
                out=half_h0_minus_h1[g][:], lhsT=minus_half[:], rhs=h_sb[g][:, 1, :], start=False, stop=True
            )

        def mix_tokens_0_and_1(g):
            mix[g] = work.tile([P, H], F32, name="mix")
            nc.vector.scalar_tensor_tensor(
                out=mix[g][:],
                in0=tanh1[g][:],
                scalar=1.0,
                in1=half_h0_minus_h1[g][:],
                op0=ALU.add,
                op1=ALU.mult,
            )

        def distance_to_token_2(g):
            nc.vector.tensor_tensor(
                out=rest[g][:], in0=h2_minus_h1[g][:], in1=mix[g][:], op=ALU.subtract
            )

        def difference_2_1(g):
            h2_minus_h1[g] = single.tile([P, H], F32, name="h2_minus_h1")
            engine = nc.vector if g in WITHOUT_PSUM_TIME else nc.gpsimd
            engine.tensor_tensor(
                out=h2_minus_h1[g][:], in0=h_sb[g][:, 2, :], in1=h_sb[g][:, 1, :], op=ALU.subtract
            )

        def logarithm(groups):
            nc.scalar.activation(
                out=abs_tanh_all[:, groups],
                in_=abs_tanh_all[:, groups],
                func=AF.Ln,
                scale=0.5,
                bias=half[:],
            )

        def combine(groups):
            nc.vector.tensor_tensor(
                out=logit2_all[:, groups],
                in0=logit2_all[:, groups],
                in1=abs_tanh_all[:, groups],
                op=ALU.add,
            )

        def second_tanh(groups):
            nc.scalar.activation(
                out=logit2_all[:, groups], in_=logit2_all[:, groups], func=AF.Tanh, scale=0.5
            )

        def weigh(groups, columns):
            nc.vector.scalar_tensor_tensor(
                out=rest_all[:, groups, columns],
                in0=logit2_all[:, groups, columns],
                scalar=-1.0,
                in1=rest_all[:, groups, columns],
                op0=ALU.add,
                op1=ALU.mult,
            )

        def store(groups, columns):
            nc.vector.scalar_tensor_tensor(
                out=rest_all[:, groups, columns],
                in0=rest_all[:, groups, columns],
                scalar=0.5,
                in1=h_all[:, groups, 2, columns],
                op0=ALU.mult,
                op1=ALU.add,
            )
            nc.sync.dma_start(
                out=out_groups[:, groups, columns], in_=rest_all[:, groups, columns]
            )

        def finish(pieces):
            for piece, before in zip(pieces + [None], [None] + pieces):
                if piece:
                    weigh(*piece)
                if before:
                    store(*before)

        def run(stage, g):
            if 0 <= g < N_GROUPS:
                stage(g)

        for t in range(-H_AHEAD, N_GROUPS + 1):
            if t > H_AHEAD:
                run(difference_2_1, t - 3)
            run(mix_tokens_0_and_1, t - 3)
            run(hidden_tokens_0_2, t)
            run(hidden_token_1, t)
            run(second_matmul, t - 2)
            run(absolute_tanh, t - 3)
            run(compare_0_1, t - 2)
            run(compare_2, t - 2)
            run(transpose_h, t + H_AHEAD)
            if t < N_GROUPS:
                open_turn(t)
            run(group_h, t + H_AHEAD)
            if t > -H_AHEAD:
                quantise(t - 1)
            run(first_matmul, t + 1)
            if t == -1:
                difference_2_1(0)
            run(group_f, t)
            run(distance_to_token_2, t - 3)
            run(half_difference_0_1, t - 2)

        all_columns = slice(0, H)
        early = [slice(g, g + 2) for g in range(0, EARLY, 2)]
        late = [slice(g, g + 2) for g in range(EARLY, N_GROUPS, 2)]
        last = N_GROUPS - 1
        difference_2_1(last - 1)
        mix_tokens_0_and_1(last - 1)
        second_matmul(last)
        absolute_tanh(last - 1)
        distance_to_token_2(last - 1)
        half_difference_0_1(last)
        for groups in early:
            logarithm(groups)
            combine(groups)
        compare_0_1(last)
        compare_2(last)
        difference_2_1(last)
        mix_tokens_0_and_1(last)
        for groups in early:
            second_tanh(groups)
        absolute_tanh(last)
        for groups in late:
            logarithm(groups)
        distance_to_token_2(last)
        finish([(groups, all_columns) for groups in early])
        for groups in late:
            combine(groups)
        one_by_one = [slice(EARLY, EARLY + 1), slice(EARLY + 1, EARLY + 2)]
        for groups in one_by_one + late[1:]:
            second_tanh(groups)
        finish(
            [(groups, all_columns) for groups in one_by_one + late[1:-1]]
            + [(slice(last - 1, last), all_columns)]
            + [(slice(last, last + 1), slice(0, H // 2)), (slice(last, last + 1), slice(H // 2, H))]
        )
